import numpy as np
import ml_dtypes


BF16 = ml_dtypes.bfloat16


def bf(x):
    return np.asarray(x, np.float32).astype(BF16)


def f64(x):
    return np.asarray(x).astype(np.float64)


E2M1 = np.array([0.0, 0.5, 1.0, 1.5, 2.0, 3.0, 4.0, 6.0, -0.0, -0.5, -1.0, -1.5, -2.0, -3.0, -4.0, -6.0])


def pack_weight(w, fmt):
    k, n = w.shape
    w = f64(bf(w)).reshape(k // 32, 32, n)
    amax = np.abs(w).max(1)
    if fmt == "e4m3":
        byte = np.frexp(amax)[1] - 1 + 127 - 7
    else:
        mant, ex = np.frexp(amax / 6.0)
        byte = np.where(mant > 0.5, ex, ex - 1) + 127
    byte = np.clip(np.where(amax > 0, byte, 1), 1, 254)
    scaled = (w * np.exp2(127.0 - byte)[:, None, :]).reshape(k, n).astype(np.float32)
    by_word = np.ascontiguousarray(scaled.reshape(k // 512, 128, 4, n).transpose(0, 1, 3, 2))
    if fmt == "e4m3":
        words = by_word.astype(ml_dtypes.float8_e4m3fn).view(np.uint8)
    else:
        c = by_word.astype(ml_dtypes.float4_e2m1fn).view(np.uint8) & 0xF
        words = c[..., 0::2] | (c[..., 1::2] << 4)
    return np.ascontiguousarray(words), np.ascontiguousarray(byte.astype(np.uint8).reshape(k // 512, 16, n))


def unpack_weight(words, scales, fmt):
    g, p, n, _ = words.shape
    if fmt == "e4m3":
        vals = np.ascontiguousarray(words).view(ml_dtypes.float8_e4m3fn).astype(np.float64)
    else:
        nib = np.empty((g, p, n, 4), np.uint8)
        nib[..., 0::2] = words & 0xF
        nib[..., 1::2] = words >> 4
        vals = E2M1[nib]
    vals = vals * np.repeat(np.exp2(scales.astype(np.float64) - 127.0), 8, axis=1)[..., None]
    return vals.transpose(0, 1, 3, 2).reshape(g * 512, n)

def pack4(w):
    words, scales = pack_weight(w, "e2m1")
    return words.reshape(words.shape[0], 128, -1), scales


def unpack4(words, scales):
    return unpack_weight(words.reshape(words.shape[0], 128, -1, 2), scales, "e2m1")


def kspread(k):
    return np.exp2(np.repeat(np.random.randint(-6, 7, k // 32), 32).astype(np.float64))


B, L_IMG, L_TXT, DM, H, D = 1, 512, 256, 2048, 8, 128
L = L_TXT + L_IMG
HD = H * D
EPS = 1e-6


def rms(x, gain):
    return x / np.sqrt(np.mean(np.square(x), axis=-1, keepdims=True) + EPS) * gain


def qkv(x, w, qn, kn):
    y = (x @ w).reshape(x.shape[0], x.shape[1], 3, H, D)
    return rms(y[:, :, 0], qn), rms(y[:, :, 1], kn), y[:, :, 2]


def rope(x, fc):
    x_ = x.reshape(x.shape[:-1] + (D // 2, 1, 2))
    out = fc[:, None, :, :, 0] * x_[..., 0] + fc[:, None, :, :, 1] * x_[..., 1]
    return out.reshape(x.shape)


def setup_inputs():
    s_i = kspread(DM)
    s_e = kspread(DM)
    r = np.random.standard_normal
    hidden_states = r((B, L_IMG, DM)) * s_i
    encoder_hidden_states = r((B, L_TXT, DM)) * s_e
    hidden_states_words, hidden_states_scales = pack4(hidden_states.reshape(B * L_IMG, DM).T)
    encoder_hidden_states_words, encoder_hidden_states_scales = pack4(encoder_hidden_states.reshape(B * L_TXT, DM).T)
    image_rotary_emb = bf(r((L, D // 2, 4)) * 0.6)
    iqkv_words, iqkv_scales = pack4(r((DM, 3 * HD)) / np.sqrt(DM) / s_i[:, None])
    eqkv_words, eqkv_scales = pack4(r((DM, 3 * HD)) / np.sqrt(DM) / s_e[:, None])
    return {
        "hidden_states_words": hidden_states_words,
        "hidden_states_scales": hidden_states_scales,
        "encoder_hidden_states_words": encoder_hidden_states_words,
        "encoder_hidden_states_scales": encoder_hidden_states_scales,
        "image_rotary_emb": image_rotary_emb,
        "W_iqkv_words": iqkv_words,
        "W_iqkv_scales": iqkv_scales,
        "W_eqkv_words": eqkv_words,
        "W_eqkv_scales": eqkv_scales,
        "qn_scale": bf(1.0 + 0.1 * r(D)),
        "kn_scale": bf(1.0 + 0.1 * r(D)),
        "eqn_scale": bf(1.0 + 0.1 * r(D)),
        "ekn_scale": bf(1.0 + 0.1 * r(D)),
    }


def reference(hidden_states_words, hidden_states_scales, encoder_hidden_states_words, encoder_hidden_states_scales, image_rotary_emb, W_iqkv_words, W_iqkv_scales, W_eqkv_words, W_eqkv_scales, qn_scale, kn_scale, eqn_scale, ekn_scale):
    xi = unpack4(hidden_states_words, hidden_states_scales).T.reshape(B, L_IMG, DM)
    xe = unpack4(encoder_hidden_states_words, encoder_hidden_states_scales).T.reshape(B, L_TXT, DM)
    q, k, v = qkv(xi, unpack4(W_iqkv_words, W_iqkv_scales), f64(qn_scale), f64(kn_scale))
    eq, ek, ev = qkv(xe, unpack4(W_eqkv_words, W_eqkv_scales), f64(eqn_scale), f64(ekn_scale))
    q = np.concatenate((eq, q), axis=1)
    k = np.concatenate((ek, k), axis=1)
    v = np.concatenate((ev, v), axis=1)
    fc = f64(image_rotary_emb).reshape(L, D // 2, 2, 2)
    return rope(q, fc).reshape(B, L, HD), rope(k, fc).reshape(B, L, HD), v.reshape(B, L, HD)

@@ -1,0 +1,299 @@
+from contextlib import ExitStack
+
+import concourse.mybir as mybir
+
+FLOPS = 2 * 768 * 2048 * 3072
+
+F32 = mybir.dt.float32
+BF16 = mybir.dt.bfloat16
+U8 = mybir.dt.uint8
+I32 = mybir.dt.int32
+FP4 = mybir.dt.float4_e2m1fn_x4
+ACT = mybir.ActivationFunctionType
+ALU = mybir.AluOpType
+
+P = 128
+PASSES = 4
+D = 128
+EPS = 1e-6
+N_WARM = 7
+BY_R = True
+
+
+def tile_fluxattention_pa_kernel(
+    tc, xi_w, xi_s, xe_w, xe_s, rot, wi_w, wi_s, we_w, we_s, qn, kn, eqn, ekn, out_q, out_k, out_v
+):
+    nc = tc.nc
+    outs = (out_q, out_k, out_v)
+
+    with ExitStack() as ctx:
+        keep = ctx.enter_context(tc.tile_pool(name="keep", bufs=1))
+        work = ctx.enter_context(tc.tile_pool(name="work", bufs=3))
+        psum = ctx.enter_context(tc.psum_pool(name="psum", bufs=8))
+        ctx.enter_context(tc.manual_schedule())
+
+        def flat(t):
+            return t[:].rearrange("p g n -> p (g n)")
+
+        def zero_v(t):
+            nc.vector.memset(flat(t).bitcast(I32), 0)
+
+        def zero_g(t):
+            nc.gpsimd.memset(flat(t).bitcast(F32), 0.0)
+
+        def load_words(dst, src, lo, hi):
+            nc.sync.dma_start(
+                out=dst[:].bitcast(I32),
+                in_=src[:, :, lo:hi].rearrange("g p n -> p g n").bitcast(I32),
+            )
+
+        def load_plane(dst, src, lo, hi):
+            for q in range(4):
+                if BY_R:
+                    nc.sync.dma_start(
+                        out=dst[q : P : 32, :, :].bitcast(I32),
+                        in_=src[:, q : 16 : 4, lo:hi].rearrange("g r n -> r g n").bitcast(I32),
+                    )
+                else:
+                    nc.sync.dma_start(
+                        out=dst[32 * q : 32 * q + 4, :, :].bitcast(I32),
+                        in_=src[:, 4 * q : 4 * q + 4, lo:hi].rearrange("g r n -> r g n").bitcast(I32),
+                    )
+
+        xw = [
+            keep.tile([P, PASSES, 512], U8, name="xw_e", tag="xw_e", align_bytes=64),
+            keep.tile([P, PASSES, 1024], U8, name="xw_i", tag="xw_i", align_bytes=64),
+        ]
+        xs = [
+            keep.tile([P, PASSES, 256], U8, name="xs_e", tag="xs_e", align_bytes=64),
+            keep.tile([P, PASSES, 512], U8, name="xs_i", tag="xs_i", align_bytes=64),
+        ]
+        ww_eq = [
+            keep.tile([P, PASSES, 1024], U8, name="ww_eq0", tag="ww_eq0", align_bytes=64),
+            keep.tile([P, PASSES, 1024], U8, name="ww_eq1", tag="ww_eq1", align_bytes=64),
+        ]
+        ww = {}
+        ws = {}
+        for s in range(2):
+            for w in range(3):
+                if (s, w) != (0, 0):
+                    nm = "ww_%d_%d" % (s, w)
+                    ww[(s, w)] = keep.tile([P, PASSES, 2048], U8, name=nm, tag=nm, align_bytes=64)
+                nm = "ws_%d_%d" % (s, w)
+                ws[(s, w)] = keep.tile([P, PASSES, 1024], U8, name=nm, tag=nm, align_bytes=64)
+        rot_sb = keep.tile([P, 6, 256], BF16, name="rot_sb", tag="rot_sb")
+        tabs = {}
+        for n in range(6):
+            for w in range(2):
+                nm = "tab_%d_%d" % (n, w)
+                tabs[(n, w)] = keep.tile([P, 2 * D], F32, name=nm, tag=nm)
+        one = keep.tile([P, 1], F32, name="one", tag="one")
+        one_out = keep.tile([P, 1], F32, name="one_out", tag="one_out")
+        ones_bf = keep.tile([P, P], BF16, name="ones_bf", tag="ones_bf")
+        warm_rhs = keep.tile([P, 512], BF16, name="warm_rhs", tag="warm_rhs")
+        gain_rows = keep.tile([P, 512], BF16, name="gain_rows", tag="gain_rows")
+        gain_all = psum.tile([P, 512], F32, name="gain_all", tag="acc")
+        warm_out = psum.tile([P, 512], F32, name="warm_out", tag="acc")
+
+        def table(n, w):
+            s = 0 if n < 2 else 1
+            j = 2 * s + w
+            nc.vector.tensor_tensor(
+                out=tabs[(n, w)][:].rearrange("p (i b a) -> p i b a", b=2, a=2),
+                in0=rot_sb[:, n, :].rearrange("p (i a b) -> p i b a", a=2, b=2),
+                in1=gain_all[:, D * j : D * j + D]
+                .rearrange("p (i b o) -> p i b o", b=2, o=1)
+                .to_broadcast([P, 64, 2, 2]),
+                op=ALU.mult,
+            )
+
+        nc.gpsimd.memset(gain_rows[:].bitcast(F32), 0.0)
+        nc.gpsimd.dma_start(out=rot_sb[:], in_=rot.rearrange("(n p) i c -> p n (i c)", p=P))
+        nc.gpsimd.memset(ones_bf[:], 1.0)
+        nc.gpsimd.memset(warm_rhs[:].bitcast(F32), 0.0)
+        zero_v(xs[0])
+        zero_v(ws[(0, 0)])
+        nc.vector.memset(one[:], 1.0)
+        nc.scalar.activation(out=one_out[:], in_=one[:], func=ACT.Abs_reciprocal_sqrt)
+
+        load_words(xw[0], xe_w, 0, 512)
+        load_words(ww_eq[0], we_w, 0, 1024)
+        for j, g in enumerate((eqn, ekn, qn, kn)):
+            nc.sync.dma_start(
+                out=gain_rows[j : j + 1, D * j : D * j + D], in_=g.rearrange("(o d) -> o d", o=1)
+            )
+        load_plane(xs[0], xe_s, 0, 256)
+        load_plane(ws[(0, 0)], we_s, 0, 1024)
+        nc.tensor.matmul(out=gain_all[:], lhsT=ones_bf[:], rhs=gain_rows[:], start=True, stop=True)
+        for i in range(N_WARM):
+            nc.tensor.matmul(out=warm_out[:], lhsT=ones_bf[:], rhs=warm_rhs[:], start=True, stop=True)
+        load_words(ww_eq[1], we_w, 1024, 2048)
+        for w in (1, 2):
+            zero_v(ws[(0, w)])
+            load_words(ww[(0, w)], we_w, 2048 * w, 2048 * w + 2048)
+            load_plane(ws[(0, w)], we_s, 1024 * w, 1024 * w + 1024)
+        zero_g(xs[1])
+        load_words(xw[1], xi_w, 0, 1024)
+        load_plane(xs[1], xi_s, 0, 512)
+        for w in (0, 2, 1):
+            zero_g(ws[(1, w)])
+            load_words(ww[(1, w)], wi_w, 2048 * w, 2048 * w + 2048)
+            load_plane(ws[(1, w)], wi_s, 1024 * w, 1024 * w + 1024)
+        for n, w in ((0, 0), (1, 0), (0, 1), (1, 1)):
+            table(n, w)
+        for n in range(2, 6):
+            for w in range(2):
+                table(n, w)
+
+        groups = [(0, 0), (1, 0), (0, 1), (1, 1), (0, 2), (1, 2)]
+        groups.extend([(2, 0), (3, 0), (4, 0), (5, 0), (2, 2), (2, 1), (3, 1), (3, 2)])
+        groups.extend([(4, 1), (5, 1), (4, 2), (5, 2)])
+        last = len(groups) - 1
+        last_heavy = max([k for k in range(len(groups)) if groups[k][1] != 2])
+
+        def matmuls(k):
+            n, w = groups[k]
+            s = 0 if n < 2 else 1
+            lt = n - 2 * s
+            banks = []
+            pieces = [(0, 512), (512, 512)] if k != last else [(0, 512), (512, 256), (768, 256)]
+            for c0, cn in pieces:
+                acc = psum.tile([P, cn], F32, name="acc", tag="acc")
+                if (s, w) == (0, 0):
+                    wt, off = ww_eq[c0 // 512], 0
+                else:
+                    wt, off = ww[(s, w)], 2 * c0
+                for g in range(PASSES):
+                    nc.tensor.matmul_mx(
+                        out=acc[:],
+                        lhsT=xw[s][:, g, 256 * lt : 256 * lt + 256].bitcast(FP4),
+                        lhsT_scale=xs[s][:, g, 128 * lt : 128 * lt + 128],
+                        rhs=wt[:, g, off : off + 2 * cn].bitcast(FP4),
+                        rhs_scale=ws[(s, w)][:, g, c0 : c0 + cn],
+                        start=(g == 0),
+                        stop=(g == PASSES - 1),
+                    )
+                banks.append(acc)
+            return banks
+
+        def store(k, o, lo, hi):
+            n, w = groups[k]
+            nc.sync.dma_start(out=outs[w][0, P * n : P * n + P, lo:hi], in_=o[:, lo:hi])
+
+        pending = []
+        late_stores = []
+        tail_heavy = [k for k in range(len(groups)) if groups[k][1] != 2][-2:]
+
+        def flush(k):
+            ready = [e for e in pending if e[0] <= k - 2]
+            for e in ready:
+                e[1]()
+                pending.remove(e)
+
+        def light(k, banks):
+            o = work.tile([P, 1024], F32, name="o", tag="o", bufs=12)
+            if k != last:
+                nc.scalar.copy(out=o[:, 0:512], in_=banks[0][:])
+                nc.vector.tensor_copy(out=o[:, 512:1024], in_=banks[1][:])
+                store(k, o, 0, 1024)
+                flush(k)
+                for e in late_stores:
+                    store(e[0], e[1], e[2], e[3])
+                late_stores.clear()
+                return
+            nc.scalar.copy(out=o[:, 0:512], in_=banks[0][:])
+            store(k, o, 0, 512)
+            nc.vector.tensor_copy(out=o[:, 512:768], in_=banks[1][:])
+            store(k, o, 512, 768)
+            nc.scalar.copy(out=o[:, 768:1024], in_=banks[2][:])
+            store(k, o, 768, 1024)
+
+        def heavy_group(k, banks):
+            n, w = groups[k]
+            tab = tabs[(n, w)]
+            ss = work.tile([P, 8], F32, name="ss", tag="ss", bufs=4)
+            r = work.tile([P, 8], F32, name="r", tag="r", bufs=4)
+            junk = work.tile([P, 8, D], BF16, name="junk", tag="junk", bufs=2)
+            pr = work.tile([P, 8, 2 * D], F32, name="pr", tag="pr")
+            o = work.tile([P, 1024], F32, name="o", tag="o", bufs=12)
+
+            def squares(half):
+                for h in range(4):
+                    j = 4 * half + h
+                    nc.scalar.activation(
+                        out=junk[:, j, :],
+                        in_=banks[half][:, D * h : D * h + D],
+                        func=ACT.Square,
+                        accum_out=ss[:, j : j + 1],
+                    )
+
+            def rstd(h0, h1):
+                nc.scalar.activation(
+                    out=r[:, h0:h1], in_=ss[:, h0:h1], func=ACT.Abs_reciprocal_sqrt, bias=EPS, scale=1.0 / D
+                )
+
+            def products_scaled(half):
+                for h in range(4):
+                    j = 4 * half + h
+                    nc.vector.scalar_tensor_tensor(
+                        out=pr[:, j, :].rearrange("p (c a) -> p c a", a=2),
+                        in0=tab[:].rearrange("p (c a) -> p c a", a=2),
+                        scalar=r[:, j : j + 1],
+                        in1=banks[half][:, D * h : D * h + D]
+                        .rearrange("p (c o) -> p c o", o=1)
+                        .to_broadcast([P, D, 2]),
+                        op0=ALU.mult,
+                        op1=ALU.mult,
+                    )
+
+            def add(h0, h1):
+                prv = pr[:, h0:h1, :].rearrange("p h (i b a) -> p (h i) b a", b=2, a=2)
+                nc.gpsimd.tensor_tensor(
+                    out=o[:, D * h0 : D * h1].rearrange("p (m a) -> p m a", a=2),
+                    in0=prv[:, :, 0, :],
+                    in1=prv[:, :, 1, :],
+                    op=ALU.add,
+                )
+
+            def finish():
+                for h in range(4):
+                    nc.scalar.activation(
+                        out=o[:, D * h : D * h + D],
+                        in_=o[:, D * h : D * h + D],
+                        func=ACT.Copy,
+                        scale=r[:, h : h + 1],
+                    )
+                store(k, o, 0, 1024)
+
+            if k in tail_heavy:
+                for half in range(2):
+                    squares(half)
+                    rstd(4 * half, 4 * half + 4)
+                    products_scaled(half)
+                    add(4 * half, 4 * half + 4)
+                    if k == last_heavy:
+                        late_stores.append((k, o, 512 * half, 512 * half + 512))
+                    else:
+                        store(k, o, 512 * half, 512 * half + 512)
+                flush(k)
+                return
+            squares(0)
+            nc.vector.tensor_tensor(
+                out=pr[:, 0:4, :].rearrange("p h (c a) -> p h c a", a=2),
+                in0=tab[:].rearrange("p (o c a) -> p o c a", o=1, a=2).to_broadcast([P, 4, D, 2]),
+                in1=banks[0][:].rearrange("p (h c o) -> p h c o", h=4, o=1).to_broadcast([P, 4, D, 2]),
+                op=ALU.mult,
+            )
+            squares(1)
+            rstd(0, 8)
+            products_scaled(1)
+            flush(k)
+            add(0, 8)
+            pending.append((k, finish))
+
+        for k in range(len(groups)):
+            banks = matmuls(k)
+            if groups[k][1] == 2:
+                light(k, banks)
+            else:
+                heavy_group(k, banks)

@@ -60,23 +60,24 @@ def tile_fluxattention_pa_kernel(
                         in_=src[:, 4 * q : 4 * q + 4, lo:hi].rearrange("g r n -> r g n").bitcast(I32),
                     )
 
-        xw = [
-            keep.tile([P, PASSES, 512], U8, name="xw_e", tag="xw_e", align_bytes=64),
-            keep.tile([P, PASSES, 1024], U8, name="xw_i", tag="xw_i", align_bytes=64),
+        xw_e = keep.tile([P, PASSES, 512], U8, name="xw_e", tag="xw_e", align_bytes=64)
+        xw_i = [
+            keep.tile([P, PASSES, 512], U8, name="xw_i0", tag="xw_i0", align_bytes=64),
+            keep.tile([P, PASSES, 512], U8, name="xw_i1", tag="xw_i1", align_bytes=64),
         ]
         xs = [
             keep.tile([P, PASSES, 256], U8, name="xs_e", tag="xs_e", align_bytes=64),
             keep.tile([P, PASSES, 512], U8, name="xs_i", tag="xs_i", align_bytes=64),
         ]
-        ww_eq = [
-            keep.tile([P, PASSES, 1024], U8, name="ww_eq0", tag="ww_eq0", align_bytes=64),
-            keep.tile([P, PASSES, 1024], U8, name="ww_eq1", tag="ww_eq1", align_bytes=64),
+        ww_iq = [
+            keep.tile([P, PASSES, 1024], U8, name="ww_iq0", tag="ww_iq0", align_bytes=64),
+            keep.tile([P, PASSES, 1024], U8, name="ww_iq1", tag="ww_iq1", align_bytes=64),
         ]
         ww = {}
         ws = {}
         for s in range(2):
             for w in range(3):
-                if (s, w) != (0, 0):
+                if (s, w) != (1, 0):
                     nm = "ww_%d_%d" % (s, w)
                     ww[(s, w)] = keep.tile([P, PASSES, 2048], U8, name=nm, tag=nm, align_bytes=64)
                 nm = "ws_%d_%d" % (s, w)
@@ -111,43 +112,48 @@ def tile_fluxattention_pa_kernel(
         nc.gpsimd.dma_start(out=rot_sb[:], in_=rot.rearrange("(n p) i c -> p n (i c)", p=P))
         nc.gpsimd.memset(ones_bf[:], 1.0)
         nc.gpsimd.memset(warm_rhs[:].bitcast(F32), 0.0)
-        zero_v(xs[0])
-        zero_v(ws[(0, 0)])
+        zero_v(xs[1])
+        zero_v(ws[(1, 0)])
         nc.vector.memset(one[:], 1.0)
         nc.scalar.activation(out=one_out[:], in_=one[:], func=ACT.Abs_reciprocal_sqrt)
 
-        load_words(xw[0], xe_w, 0, 512)
-        load_words(ww_eq[0], we_w, 0, 1024)
+        load_words(xw_i[0], xi_w, 0, 512)
+        load_words(ww_iq[0], wi_w, 0, 1024)
         for j, g in enumerate((eqn, ekn, qn, kn)):
             nc.sync.dma_start(
                 out=gain_rows[j : j + 1, D * j : D * j + D], in_=g.rearrange("(o d) -> o d", o=1)
             )
-        load_plane(xs[0], xe_s, 0, 256)
-        load_plane(ws[(0, 0)], we_s, 0, 1024)
+        load_plane(xs[1], xi_s, 0, 512)
+        load_plane(ws[(1, 0)], wi_s, 0, 1024)
         nc.tensor.matmul(out=gain_all[:], lhsT=ones_bf[:], rhs=gain_rows[:], start=True, stop=True)
         for i in range(N_WARM):
             nc.tensor.matmul(out=warm_out[:], lhsT=ones_bf[:], rhs=warm_rhs[:], start=True, stop=True)
-        load_words(ww_eq[1], we_w, 1024, 2048)
-        for w in (1, 2):
-            zero_v(ws[(0, w)])
-            load_words(ww[(0, w)], we_w, 2048 * w, 2048 * w + 2048)
-            load_plane(ws[(0, w)], we_s, 1024 * w, 1024 * w + 1024)
-        zero_g(xs[1])
-        load_words(xw[1], xi_w, 0, 1024)
-        load_plane(xs[1], xi_s, 0, 512)
-        for w in (0, 2, 1):
-            zero_g(ws[(1, w)])
+        load_words(ww_iq[1], wi_w, 1024, 2048)
+        load_words(xw_i[1], xi_w, 512, 1024)
+        for w in (2, 1):
+            zero_v(ws[(1, w)])
             load_words(ww[(1, w)], wi_w, 2048 * w, 2048 * w + 2048)
             load_plane(ws[(1, w)], wi_s, 1024 * w, 1024 * w + 1024)
-        for n, w in ((0, 0), (1, 0), (0, 1), (1, 1)):
-            table(n, w)
-        for n in range(2, 6):
-            for w in range(2):
+        zero_g(xs[0])
+        for w in range(3):
+            zero_g(ws[(0, w)])
+        for w in range(2):
+            for n in range(2, 6):
+                table(n, w)
+        for w in range(2):
+            for n in range(2):
                 table(n, w)
 
-        groups = [(0, 0), (1, 0), (0, 1), (1, 1), (0, 2), (1, 2)]
-        groups.extend([(2, 0), (3, 0), (4, 0), (5, 0), (2, 2), (2, 1), (3, 1), (3, 2)])
-        groups.extend([(4, 1), (5, 1), (4, 2), (5, 2)])
+        def load_text_x():
+            load_words(xw_e, xe_w, 0, 512)
+            load_plane(xs[0], xe_s, 0, 256)
+
+        def load_text_w(w):
+            load_words(ww[(0, w)], we_w, 2048 * w, 2048 * w + 2048)
+            load_plane(ws[(0, w)], we_s, 1024 * w, 1024 * w + 1024)
+
+        groups = [(2, 0), (3, 0), (4, 0), (5, 0), (2, 2), (2, 1), (3, 1), (3, 2), (4, 1), (5, 1), (4, 2)]
+        groups.extend([(0, 0), (1, 0), (5, 2), (0, 1), (1, 1), (0, 2), (1, 2)])
         last = len(groups) - 1
         last_heavy = max([k for k in range(len(groups)) if groups[k][1] != 2])
 
@@ -159,14 +165,18 @@ def tile_fluxattention_pa_kernel(
             pieces = [(0, 512), (512, 512)] if k != last else [(0, 512), (512, 256), (768, 256)]
             for c0, cn in pieces:
                 acc = psum.tile([P, cn], F32, name="acc", tag="acc")
-                if (s, w) == (0, 0):
-                    wt, off = ww_eq[c0 // 512], 0
+                if (s, w) == (1, 0):
+                    wt, off = ww_iq[c0 // 512], 0
                 else:
                     wt, off = ww[(s, w)], 2 * c0
+                if s == 0:
+                    xt, xo = xw_e, 256 * lt
+                else:
+                    xt, xo = xw_i[lt // 2], 256 * (lt % 2)
                 for g in range(PASSES):
                     nc.tensor.matmul_mx(
                         out=acc[:],
-                        lhsT=xw[s][:, g, 256 * lt : 256 * lt + 256].bitcast(FP4),
+                        lhsT=xt[:, g, xo : xo + 256].bitcast(FP4),
                         lhsT_scale=xs[s][:, g, 128 * lt : 128 * lt + 128],
                         rhs=wt[:, g, off : off + 2 * cn].bitcast(FP4),
                         rhs_scale=ws[(s, w)][:, g, c0 : c0 + cn],
@@ -297,3 +307,10 @@ def tile_fluxattention_pa_kernel(
                 light(k, banks)
             else:
                 heavy_group(k, banks)
+            if k == 3:
+                load_text_x()
+                load_text_w(0)
+            if k == 6:
+                load_text_w(1)
+            if k == 9:
+                load_text_w(2)

@@ -307,10 +307,10 @@ def tile_fluxattention_pa_kernel(
                 light(k, banks)
             else:
                 heavy_group(k, banks)
-            if k == 3:
+            if k == 1:
                 load_text_x()
                 load_text_w(0)
-            if k == 6:
+            if k == 3:
                 load_text_w(1)
-            if k == 9:
+            if k == 5:
                 load_text_w(2)

@@ -16,7 +16,8 @@ P = 128
 PASSES = 4
 D = 128
 EPS = 1e-6
-N_WARM = 7
+N_WARM_A = 4
+N_WARM_B = 5
 BY_R = True
 
 
@@ -110,10 +111,10 @@ def tile_fluxattention_pa_kernel(
 
         nc.gpsimd.memset(gain_rows[:].bitcast(F32), 0.0)
         nc.gpsimd.dma_start(out=rot_sb[:], in_=rot.rearrange("(n p) i c -> p n (i c)", p=P))
-        nc.gpsimd.memset(ones_bf[:], 1.0)
-        nc.gpsimd.memset(warm_rhs[:].bitcast(F32), 0.0)
         zero_v(xs[1])
         zero_v(ws[(1, 0)])
+        nc.vector.memset(ones_bf[:], 1.0)
+        nc.vector.memset(warm_rhs[:].bitcast(I32), 0)
         nc.vector.memset(one[:], 1.0)
         nc.scalar.activation(out=one_out[:], in_=one[:], func=ACT.Abs_reciprocal_sqrt)
 
@@ -125,8 +126,10 @@ def tile_fluxattention_pa_kernel(
             )
         load_plane(xs[1], xi_s, 0, 512)
         load_plane(ws[(1, 0)], wi_s, 0, 1024)
+        for i in range(N_WARM_A):
+            nc.tensor.matmul(out=warm_out[:], lhsT=ones_bf[:], rhs=warm_rhs[:], start=True, stop=True)
         nc.tensor.matmul(out=gain_all[:], lhsT=ones_bf[:], rhs=gain_rows[:], start=True, stop=True)
-        for i in range(N_WARM):
+        for i in range(N_WARM_B):
             nc.tensor.matmul(out=warm_out[:], lhsT=ones_bf[:], rhs=warm_rhs[:], start=True, stop=True)
         load_words(ww_iq[1], wi_w, 1024, 2048)
         load_words(xw_i[1], xi_w, 512, 1024)

@@ -16,8 +16,8 @@ P = 128
 PASSES = 4
 D = 128
 EPS = 1e-6
-N_WARM_A = 4
-N_WARM_B = 5
+N_WARM_A = 32
+N_WARM_B = 26
 BY_R = True
 
 
@@ -92,10 +92,9 @@ def tile_fluxattention_pa_kernel(
         one = keep.tile([P, 1], F32, name="one", tag="one")
         one_out = keep.tile([P, 1], F32, name="one_out", tag="one_out")
         ones_bf = keep.tile([P, P], BF16, name="ones_bf", tag="ones_bf")
-        warm_rhs = keep.tile([P, 512], BF16, name="warm_rhs", tag="warm_rhs")
         gain_rows = keep.tile([P, 512], BF16, name="gain_rows", tag="gain_rows")
         gain_all = psum.tile([P, 512], F32, name="gain_all", tag="acc")
-        warm_out = psum.tile([P, 512], F32, name="warm_out", tag="acc")
+        warm_out = psum.tile([P, P], F32, name="warm_out", tag="acc")
 
         def table(n, w):
             s = 0 if n < 2 else 1
@@ -111,10 +110,9 @@ def tile_fluxattention_pa_kernel(
 
         nc.gpsimd.memset(gain_rows[:].bitcast(F32), 0.0)
         nc.gpsimd.dma_start(out=rot_sb[:], in_=rot.rearrange("(n p) i c -> p n (i c)", p=P))
+        nc.vector.memset(ones_bf[:], 1.0)
         zero_v(xs[1])
         zero_v(ws[(1, 0)])
-        nc.vector.memset(ones_bf[:], 1.0)
-        nc.vector.memset(warm_rhs[:].bitcast(I32), 0)
         nc.vector.memset(one[:], 1.0)
         nc.scalar.activation(out=one_out[:], in_=one[:], func=ACT.Abs_reciprocal_sqrt)
 
@@ -127,10 +125,10 @@ def tile_fluxattention_pa_kernel(
         load_plane(xs[1], xi_s, 0, 512)
         load_plane(ws[(1, 0)], wi_s, 0, 1024)
         for i in range(N_WARM_A):
-            nc.tensor.matmul(out=warm_out[:], lhsT=ones_bf[:], rhs=warm_rhs[:], start=True, stop=True)
+            nc.tensor.matmul(out=warm_out[:], lhsT=ones_bf[:], rhs=ones_bf[:], start=True, stop=True)
         nc.tensor.matmul(out=gain_all[:], lhsT=ones_bf[:], rhs=gain_rows[:], start=True, stop=True)
         for i in range(N_WARM_B):
-            nc.tensor.matmul(out=warm_out[:], lhsT=ones_bf[:], rhs=warm_rhs[:], start=True, stop=True)
+            nc.tensor.matmul(out=warm_out[:], lhsT=ones_bf[:], rhs=ones_bf[:], start=True, stop=True)
         load_words(ww_iq[1], wi_w, 1024, 2048)
         load_words(xw_i[1], xi_w, 512, 1024)
         for w in (2, 1):

@@ -17,8 +17,7 @@ PASSES = 4
 D = 128
 EPS = 1e-6
 N_WARM_A = 32
-N_WARM_B = 26
-BY_R = True
+N_WARM_B = 22
 
 
 def tile_fluxattention_pa_kernel(
@@ -49,26 +48,22 @@ def tile_fluxattention_pa_kernel(
             )
 
         def load_plane(dst, src, lo, hi):
-            for q in range(4):
-                if BY_R:
-                    nc.sync.dma_start(
-                        out=dst[q : P : 32, :, :].bitcast(I32),
-                        in_=src[:, q : 16 : 4, lo:hi].rearrange("g r n -> r g n").bitcast(I32),
-                    )
-                else:
-                    nc.sync.dma_start(
-                        out=dst[32 * q : 32 * q + 4, :, :].bitcast(I32),
-                        in_=src[:, 4 * q : 4 * q + 4, lo:hi].rearrange("g r n -> r g n").bitcast(I32),
-                    )
+            for r in range(4):
+                nc.sync.dma_start(
+                    out=dst[r : P : 32, :, :].bitcast(I32),
+                    in_=src[:, r : 16 : 4, lo:hi].rearrange("g r n -> r g n").bitcast(I32),
+                )
 
         xw_e = keep.tile([P, PASSES, 512], U8, name="xw_e", tag="xw_e", align_bytes=64)
         xw_i = [
             keep.tile([P, PASSES, 512], U8, name="xw_i0", tag="xw_i0", align_bytes=64),
             keep.tile([P, PASSES, 512], U8, name="xw_i1", tag="xw_i1", align_bytes=64),
         ]
-        xs = [
-            keep.tile([P, PASSES, 256], U8, name="xs_e", tag="xs_e", align_bytes=64),
-            keep.tile([P, PASSES, 512], U8, name="xs_i", tag="xs_i", align_bytes=64),
+        xs_e = keep.tile([P, PASSES, 256], U8, name="xs_e", tag="xs_e", align_bytes=64)
+        xs_i = keep.tile([P, PASSES, 512], U8, name="xs_i", tag="xs_i", align_bytes=64)
+        ws_iq = [
+            keep.tile([P, PASSES, 512], U8, name="ws_iq0", tag="ws_iq0", align_bytes=64),
+            keep.tile([P, PASSES, 512], U8, name="ws_iq1", tag="ws_iq1", align_bytes=64),
         ]
         ww_iq = [
             keep.tile([P, PASSES, 1024], U8, name="ww_iq0", tag="ww_iq0", align_bytes=64),
@@ -81,8 +76,8 @@ def tile_fluxattention_pa_kernel(
                 if (s, w) != (1, 0):
                     nm = "ww_%d_%d" % (s, w)
                     ww[(s, w)] = keep.tile([P, PASSES, 2048], U8, name=nm, tag=nm, align_bytes=64)
-                nm = "ws_%d_%d" % (s, w)
-                ws[(s, w)] = keep.tile([P, PASSES, 1024], U8, name=nm, tag=nm, align_bytes=64)
+                    nm = "ws_%d_%d" % (s, w)
+                    ws[(s, w)] = keep.tile([P, PASSES, 1024], U8, name=nm, tag=nm, align_bytes=64)
         rot_sb = keep.tile([P, 6, 256], BF16, name="rot_sb", tag="rot_sb")
         tabs = {}
         for n in range(6):
@@ -111,10 +106,12 @@ def tile_fluxattention_pa_kernel(
         nc.gpsimd.memset(gain_rows[:].bitcast(F32), 0.0)
         nc.gpsimd.dma_start(out=rot_sb[:], in_=rot.rearrange("(n p) i c -> p n (i c)", p=P))
         nc.vector.memset(ones_bf[:], 1.0)
-        zero_v(xs[1])
-        zero_v(ws[(1, 0)])
+        zero_v(xs_i)
+        zero_v(ws_iq[0])
         nc.vector.memset(one[:], 1.0)
         nc.scalar.activation(out=one_out[:], in_=one[:], func=ACT.Abs_reciprocal_sqrt)
+
+        zero_v(ws_iq[1])
 
         load_words(xw_i[0], xi_w, 0, 512)
         load_words(ww_iq[0], wi_w, 0, 1024)
@@ -122,20 +119,21 @@ def tile_fluxattention_pa_kernel(
             nc.sync.dma_start(
                 out=gain_rows[j : j + 1, D * j : D * j + D], in_=g.rearrange("(o d) -> o d", o=1)
             )
-        load_plane(xs[1], xi_s, 0, 512)
-        load_plane(ws[(1, 0)], wi_s, 0, 1024)
+        load_plane(xs_i, xi_s, 0, 512)
+        load_plane(ws_iq[0], wi_s, 0, 512)
         for i in range(N_WARM_A):
             nc.tensor.matmul(out=warm_out[:], lhsT=ones_bf[:], rhs=ones_bf[:], start=True, stop=True)
         nc.tensor.matmul(out=gain_all[:], lhsT=ones_bf[:], rhs=gain_rows[:], start=True, stop=True)
         for i in range(N_WARM_B):
             nc.tensor.matmul(out=warm_out[:], lhsT=ones_bf[:], rhs=ones_bf[:], start=True, stop=True)
-        load_words(ww_iq[1], wi_w, 1024, 2048)
         load_words(xw_i[1], xi_w, 512, 1024)
+        load_words(ww_iq[1], wi_w, 1024, 2048)
+        load_plane(ws_iq[1], wi_s, 512, 1024)
         for w in (2, 1):
             zero_v(ws[(1, w)])
             load_words(ww[(1, w)], wi_w, 2048 * w, 2048 * w + 2048)
             load_plane(ws[(1, w)], wi_s, 1024 * w, 1024 * w + 1024)
-        zero_g(xs[0])
+        zero_g(xs_e)
         for w in range(3):
             zero_g(ws[(0, w)])
         for w in range(2):
@@ -147,40 +145,49 @@ def tile_fluxattention_pa_kernel(
 
         def load_text_x():
             load_words(xw_e, xe_w, 0, 512)
-            load_plane(xs[0], xe_s, 0, 256)
+            load_plane(xs_e, xe_s, 0, 256)
 
         def load_text_w(w):
             load_words(ww[(0, w)], we_w, 2048 * w, 2048 * w + 2048)
             load_plane(ws[(0, w)], we_s, 1024 * w, 1024 * w + 1024)
 
-        groups = [(2, 0), (3, 0), (4, 0), (5, 0), (2, 2), (2, 1), (3, 1), (3, 2), (4, 1), (5, 1), (4, 2)]
-        groups.extend([(0, 0), (1, 0), (5, 2), (0, 1), (1, 1), (0, 2), (1, 2)])
+        groups = []
+        for half in range(2):
+            for n in (2, 4):
+                groups.append((0, ((n, half), (n + 1, half))))
+        order = [(2, 2), (2, 1), (3, 1), (3, 2), (4, 1), (5, 1), (4, 2)]
+        order.extend([(0, 0), (1, 0), (5, 2), (0, 1), (1, 1), (0, 2), (1, 2)])
+        for n, w in order:
+            groups.append((w, ((n, 0), (n, 1))))
         last = len(groups) - 1
-        last_heavy = max([k for k in range(len(groups)) if groups[k][1] != 2])
+        last_heavy = max([k for k in range(len(groups)) if groups[k][0] != 2])
 
         def matmuls(k):
-            n, w = groups[k]
-            s = 0 if n < 2 else 1
-            lt = n - 2 * s
+            w, pair = groups[k]
             banks = []
-            pieces = [(0, 512), (512, 512)] if k != last else [(0, 512), (512, 256), (768, 256)]
-            for c0, cn in pieces:
+            pieces = [(n, 512 * half, 512) for n, half in pair]
+            if k == last:
+                n = pair[1][0]
+                pieces[1:] = [(n, 512, 256), (n, 768, 256)]
+            for n, c0, cn in pieces:
+                s = 0 if n < 2 else 1
+                lt = n % 2
                 acc = psum.tile([P, cn], F32, name="acc", tag="acc")
                 if (s, w) == (1, 0):
-                    wt, off = ww_iq[c0 // 512], 0
+                    wt, st, c1 = ww_iq[c0 // 512], ws_iq[c0 // 512], 0
                 else:
-                    wt, off = ww[(s, w)], 2 * c0
+                    wt, st, c1 = ww[(s, w)], ws[(s, w)], c0
                 if s == 0:
-                    xt, xo = xw_e, 256 * lt
+                    xt, xst, x0 = xw_e, xs_e, 128 * n
                 else:
-                    xt, xo = xw_i[lt // 2], 256 * (lt % 2)
+                    xt, xst, x0 = xw_i[n // 2 - 1], xs_i, 128 * (n - 2)
                 for g in range(PASSES):
                     nc.tensor.matmul_mx(
                         out=acc[:],
-                        lhsT=xt[:, g, xo : xo + 256].bitcast(FP4),
-                        lhsT_scale=xs[s][:, g, 128 * lt : 128 * lt + 128],
-                        rhs=wt[:, g, off : off + 2 * cn].bitcast(FP4),
-                        rhs_scale=ws[(s, w)][:, g, c0 : c0 + cn],
+                        lhsT=xt[:, g, 256 * lt : 256 * lt + 256].bitcast(FP4),
+                        lhsT_scale=xst[:, g, x0 : x0 + 128],
+                        rhs=wt[:, g, 2 * c1 : 2 * c1 + 2 * cn].bitcast(FP4),
+                        rhs_scale=st[:, g, c1 : c1 + cn],
                         start=(g == 0),
                         stop=(g == PASSES - 1),
                     )
@@ -188,12 +195,21 @@ def tile_fluxattention_pa_kernel(
             return banks
 
         def store(k, o, lo, hi):
-            n, w = groups[k]
+            w, pair = groups[k]
+            n, half = pair[0]
+            if pair[1][0] != n:
+                nc.sync.dma_start(
+                    out=outs[w][0, P * n : P * n + 2 * P, 512 * half : 512 * half + 512].rearrange(
+                        "(t p) c -> p t c", p=P
+                    ),
+                    in_=o[:].rearrange("p (t c) -> p t c", t=2),
+                )
+                return
             nc.sync.dma_start(out=outs[w][0, P * n : P * n + P, lo:hi], in_=o[:, lo:hi])
 
         pending = []
         late_stores = []
-        tail_heavy = [k for k in range(len(groups)) if groups[k][1] != 2][-2:]
+        tail_heavy = [k for k in range(len(groups)) if groups[k][0] != 2][-2:]
 
         def flush(k):
             ready = [e for e in pending if e[0] <= k - 2]
@@ -220,8 +236,8 @@ def tile_fluxattention_pa_kernel(
             store(k, o, 768, 1024)
 
         def heavy_group(k, banks):
-            n, w = groups[k]
-            tab = tabs[(n, w)]
+            w, pair = groups[k]
+            tab = [tabs[(n, w)] for n, half in pair]
             ss = work.tile([P, 8], F32, name="ss", tag="ss", bufs=4)
             r = work.tile([P, 8], F32, name="r", tag="r", bufs=4)
             junk = work.tile([P, 8, D], BF16, name="junk", tag="junk", bufs=2)
@@ -248,7 +264,7 @@ def tile_fluxattention_pa_kernel(
                     j = 4 * half + h
                     nc.vector.scalar_tensor_tensor(
                         out=pr[:, j, :].rearrange("p (c a) -> p c a", a=2),
-                        in0=tab[:].rearrange("p (c a) -> p c a", a=2),
+                        in0=tab[half][:].rearrange("p (c a) -> p c a", a=2),
                         scalar=r[:, j : j + 1],
                         in1=banks[half][:, D * h : D * h + D]
                         .rearrange("p (c o) -> p c o", o=1)
@@ -291,7 +307,7 @@ def tile_fluxattention_pa_kernel(
             squares(0)
             nc.vector.tensor_tensor(
                 out=pr[:, 0:4, :].rearrange("p h (c a) -> p h c a", a=2),
-                in0=tab[:].rearrange("p (o c a) -> p o c a", o=1, a=2).to_broadcast([P, 4, D, 2]),
+                in0=tab[0][:].rearrange("p (o c a) -> p o c a", o=1, a=2).to_broadcast([P, 4, D, 2]),
                 in1=banks[0][:].rearrange("p (h c o) -> p h c o", h=4, o=1).to_broadcast([P, 4, D, 2]),
                 op=ALU.mult,
             )
@@ -304,7 +320,7 @@ def tile_fluxattention_pa_kernel(
 
         for k in range(len(groups)):
             banks = matmuls(k)
-            if groups[k][1] == 2:
+            if groups[k][0] == 2:
                 light(k, banks)
             else:
                 heavy_group(k, banks)

from contextlib import ExitStack

import concourse.mybir as mybir

FLOPS = 2 * 768 * 2048 * 3072

F32 = mybir.dt.float32
BF16 = mybir.dt.bfloat16
U8 = mybir.dt.uint8
I32 = mybir.dt.int32
FP4 = mybir.dt.float4_e2m1fn_x4
ACT = mybir.ActivationFunctionType
ALU = mybir.AluOpType

P = 128
PASSES = 4
D = 128
EPS = 1e-6
N_WARM_A = 32
N_WARM_B = 22


def tile_fluxattention_pa_kernel(
    tc, xi_w, xi_s, xe_w, xe_s, rot, wi_w, wi_s, we_w, we_s, qn, kn, eqn, ekn, out_q, out_k, out_v
):
    nc = tc.nc
    outs = (out_q, out_k, out_v)

    with ExitStack() as ctx:
        keep = ctx.enter_context(tc.tile_pool(name="keep", bufs=1))
        work = ctx.enter_context(tc.tile_pool(name="work", bufs=3))
        psum = ctx.enter_context(tc.psum_pool(name="psum", bufs=8))
        ctx.enter_context(tc.manual_schedule())

        def flat(t):
            return t[:].rearrange("p g n -> p (g n)")

        def zero_v(t):
            nc.vector.memset(flat(t).bitcast(I32), 0)

        def zero_g(t):
            nc.gpsimd.memset(flat(t).bitcast(F32), 0.0)

        def load_words(dst, src, lo, hi):
            nc.sync.dma_start(
                out=dst[:].bitcast(I32),
                in_=src[:, :, lo:hi].rearrange("g p n -> p g n").bitcast(I32),
            )

        def load_plane(dst, src, lo, hi):
            for r in range(4):
                nc.sync.dma_start(
                    out=dst[r : P : 32, :, :].bitcast(I32),
                    in_=src[:, r : 16 : 4, lo:hi].rearrange("g r n -> r g n").bitcast(I32),
                )

        xw_e = keep.tile([P, PASSES, 512], U8, name="xw_e", tag="xw_e", align_bytes=64)
        xw_i = [
            keep.tile([P, PASSES, 512], U8, name="xw_i0", tag="xw_i0", align_bytes=64),
            keep.tile([P, PASSES, 512], U8, name="xw_i1", tag="xw_i1", align_bytes=64),
        ]
        xs_e = keep.tile([P, PASSES, 256], U8, name="xs_e", tag="xs_e", align_bytes=64)
        xs_i = keep.tile([P, PASSES, 512], U8, name="xs_i", tag="xs_i", align_bytes=64)
        ws_iq = [
            keep.tile([P, PASSES, 512], U8, name="ws_iq0", tag="ws_iq0", align_bytes=64),
            keep.tile([P, PASSES, 512], U8, name="ws_iq1", tag="ws_iq1", align_bytes=64),
        ]
        ww_iq = [
            keep.tile([P, PASSES, 1024], U8, name="ww_iq0", tag="ww_iq0", align_bytes=64),
            keep.tile([P, PASSES, 1024], U8, name="ww_iq1", tag="ww_iq1", align_bytes=64),
        ]
        ww = {}
        ws = {}
        for s in range(2):
            for w in range(3):
                if (s, w) != (1, 0):
                    nm = "ww_%d_%d" % (s, w)
                    ww[(s, w)] = keep.tile([P, PASSES, 2048], U8, name=nm, tag=nm, align_bytes=64)
                    nm = "ws_%d_%d" % (s, w)
                    ws[(s, w)] = keep.tile([P, PASSES, 1024], U8, name=nm, tag=nm, align_bytes=64)
        rot_sb = keep.tile([P, 6, 256], BF16, name="rot_sb", tag="rot_sb")
        tabs = {}
        for n in range(6):
            for w in range(2):
                nm = "tab_%d_%d" % (n, w)
                tabs[(n, w)] = keep.tile([P, 2 * D], F32, name=nm, tag=nm)
        one = keep.tile([P, 1], F32, name="one", tag="one")
        one_out = keep.tile([P, 1], F32, name="one_out", tag="one_out")
        ones_bf = keep.tile([P, P], BF16, name="ones_bf", tag="ones_bf")
        gain_rows = keep.tile([P, 512], BF16, name="gain_rows", tag="gain_rows")
        gain_all = psum.tile([P, 512], F32, name="gain_all", tag="acc")
        warm_out = psum.tile([P, P], F32, name="warm_out", tag="acc")

        def table(n, w):
            s = 0 if n < 2 else 1
            j = 2 * s + w
            nc.vector.tensor_tensor(
                out=tabs[(n, w)][:].rearrange("p (i b a) -> p i b a", b=2, a=2),
                in0=rot_sb[:, n, :].rearrange("p (i a b) -> p i b a", a=2, b=2),
                in1=gain_all[:, D * j : D * j + D]
                .rearrange("p (i b o) -> p i b o", b=2, o=1)
                .to_broadcast([P, 64, 2, 2]),
                op=ALU.mult,
            )

        nc.gpsimd.memset(gain_rows[:].bitcast(F32), 0.0)
        nc.gpsimd.dma_start(out=rot_sb[:], in_=rot.rearrange("(n p) i c -> p n (i c)", p=P))
        nc.vector.memset(ones_bf[:], 1.0)
        zero_v(xs_i)
        zero_v(ws_iq[0])
        nc.vector.memset(one[:], 1.0)
        nc.scalar.activation(out=one_out[:], in_=one[:], func=ACT.Abs_reciprocal_sqrt)

        zero_v(ws_iq[1])

        load_words(xw_i[0], xi_w, 0, 512)
        load_words(ww_iq[0], wi_w, 0, 1024)
        for j, g in enumerate((eqn, ekn, qn, kn)):
            nc.sync.dma_start(
                out=gain_rows[j : j + 1, D * j : D * j + D], in_=g.rearrange("(o d) -> o d", o=1)
            )
        load_plane(xs_i, xi_s, 0, 512)
        load_plane(ws_iq[0], wi_s, 0, 512)
        for i in range(N_WARM_A):
            nc.tensor.matmul(out=warm_out[:], lhsT=ones_bf[:], rhs=ones_bf[:], start=True, stop=True)
        nc.tensor.matmul(out=gain_all[:], lhsT=ones_bf[:], rhs=gain_rows[:], start=True, stop=True)
        for i in range(N_WARM_B):
            nc.tensor.matmul(out=warm_out[:], lhsT=ones_bf[:], rhs=ones_bf[:], start=True, stop=True)
        load_words(xw_i[1], xi_w, 512, 1024)
        load_words(ww_iq[1], wi_w, 1024, 2048)
        load_plane(ws_iq[1], wi_s, 512, 1024)
        for w in (2, 1):
            zero_v(ws[(1, w)])
            load_words(ww[(1, w)], wi_w, 2048 * w, 2048 * w + 2048)
            load_plane(ws[(1, w)], wi_s, 1024 * w, 1024 * w + 1024)
        zero_g(xs_e)
        for w in range(3):
            zero_g(ws[(0, w)])
        for w in range(2):
            for n in range(2, 6):
                table(n, w)
        for w in range(2):
            for n in range(2):
                table(n, w)

        def load_text_x():
            load_words(xw_e, xe_w, 0, 512)
            load_plane(xs_e, xe_s, 0, 256)

        def load_text_w(w):
            load_words(ww[(0, w)], we_w, 2048 * w, 2048 * w + 2048)
            load_plane(ws[(0, w)], we_s, 1024 * w, 1024 * w + 1024)

        groups = []
        for half in range(2):
            for n in (2, 4):
                groups.append((0, ((n, half), (n + 1, half))))
        order = [(2, 2), (2, 1), (3, 1), (3, 2), (4, 1), (5, 1), (4, 2)]
        order.extend([(0, 0), (1, 0), (5, 2), (0, 1), (1, 1), (0, 2), (1, 2)])
        for n, w in order:
            groups.append((w, ((n, 0), (n, 1))))
        last = len(groups) - 1
        last_heavy = max([k for k in range(len(groups)) if groups[k][0] != 2])

        def matmuls(k):
            w, pair = groups[k]
            banks = []
            pieces = [(n, 512 * half, 512) for n, half in pair]
            if k == last:
                n = pair[1][0]
                pieces[1:] = [(n, 512, 256), (n, 768, 256)]
            for n, c0, cn in pieces:
                s = 0 if n < 2 else 1
                lt = n % 2
                acc = psum.tile([P, cn], F32, name="acc", tag="acc")
                if (s, w) == (1, 0):
                    wt, st, c1 = ww_iq[c0 // 512], ws_iq[c0 // 512], 0
                else:
                    wt, st, c1 = ww[(s, w)], ws[(s, w)], c0
                if s == 0:
                    xt, xst, x0 = xw_e, xs_e, 128 * n
                else:
                    xt, xst, x0 = xw_i[n // 2 - 1], xs_i, 128 * (n - 2)
                for g in range(PASSES):
                    nc.tensor.matmul_mx(
                        out=acc[:],
                        lhsT=xt[:, g, 256 * lt : 256 * lt + 256].bitcast(FP4),
                        lhsT_scale=xst[:, g, x0 : x0 + 128],
                        rhs=wt[:, g, 2 * c1 : 2 * c1 + 2 * cn].bitcast(FP4),
                        rhs_scale=st[:, g, c1 : c1 + cn],
                        start=(g == 0),
                        stop=(g == PASSES - 1),
                    )
                banks.append(acc)
            return banks

        def store(k, o, lo, hi):
            w, pair = groups[k]
            n, half = pair[0]
            if pair[1][0] != n:
                nc.sync.dma_start(
                    out=outs[w][0, P * n : P * n + 2 * P, 512 * half : 512 * half + 512].rearrange(
                        "(t p) c -> p t c", p=P
                    ),
                    in_=o[:].rearrange("p (t c) -> p t c", t=2),
                )
                return
            nc.sync.dma_start(out=outs[w][0, P * n : P * n + P, lo:hi], in_=o[:, lo:hi])

        pending = []
        late_stores = []
        tail_heavy = [k for k in range(len(groups)) if groups[k][0] != 2][-2:]

        def flush(k):
            ready = [e for e in pending if e[0] <= k - 2]
            for e in ready:
                e[1]()
                pending.remove(e)

        def light(k, banks):
            o = work.tile([P, 1024], F32, name="o", tag="o", bufs=12)
            if k != last:
                nc.scalar.copy(out=o[:, 0:512], in_=banks[0][:])
                nc.vector.tensor_copy(out=o[:, 512:1024], in_=banks[1][:])
                store(k, o, 0, 1024)
                flush(k)
                for e in late_stores:
                    store(e[0], e[1], e[2], e[3])
                late_stores.clear()
                return
            nc.scalar.copy(out=o[:, 0:512], in_=banks[0][:])
            store(k, o, 0, 512)
            nc.vector.tensor_copy(out=o[:, 512:768], in_=banks[1][:])
            store(k, o, 512, 768)
            nc.scalar.copy(out=o[:, 768:1024], in_=banks[2][:])
            store(k, o, 768, 1024)

        def heavy_group(k, banks):
            w, pair = groups[k]
            tab = [tabs[(n, w)] for n, half in pair]
            ss = work.tile([P, 8], F32, name="ss", tag="ss", bufs=4)
            r = work.tile([P, 8], F32, name="r", tag="r", bufs=4)
            junk = work.tile([P, 8, D], BF16, name="junk", tag="junk", bufs=2)
            pr = work.tile([P, 8, 2 * D], F32, name="pr", tag="pr")
            o = work.tile([P, 1024], F32, name="o", tag="o", bufs=12)

            def squares(half):
                for h in range(4):
                    j = 4 * half + h
                    nc.scalar.activation(
                        out=junk[:, j, :],
                        in_=banks[half][:, D * h : D * h + D],
                        func=ACT.Square,
                        accum_out=ss[:, j : j + 1],
                    )

            def rstd(h0, h1):
                nc.scalar.activation(
                    out=r[:, h0:h1], in_=ss[:, h0:h1], func=ACT.Abs_reciprocal_sqrt, bias=EPS, scale=1.0 / D
                )

            def products_scaled(half):
                for h in range(4):
                    j = 4 * half + h
                    nc.vector.scalar_tensor_tensor(
                        out=pr[:, j, :].rearrange("p (c a) -> p c a", a=2),
                        in0=tab[half][:].rearrange("p (c a) -> p c a", a=2),
                        scalar=r[:, j : j + 1],
                        in1=banks[half][:, D * h : D * h + D]
                        .rearrange("p (c o) -> p c o", o=1)
                        .to_broadcast([P, D, 2]),
                        op0=ALU.mult,
                        op1=ALU.mult,
                    )

            def add(h0, h1):
                prv = pr[:, h0:h1, :].rearrange("p h (i b a) -> p (h i) b a", b=2, a=2)
                nc.gpsimd.tensor_tensor(
                    out=o[:, D * h0 : D * h1].rearrange("p (m a) -> p m a", a=2),
                    in0=prv[:, :, 0, :],
                    in1=prv[:, :, 1, :],
                    op=ALU.add,
                )

            def finish():
                for h in range(4):
                    nc.scalar.activation(
                        out=o[:, D * h : D * h + D],
                        in_=o[:, D * h : D * h + D],
                        func=ACT.Copy,
                        scale=r[:, h : h + 1],
                    )
                store(k, o, 0, 1024)

            if k in tail_heavy:
                for half in range(2):
                    squares(half)
                    rstd(4 * half, 4 * half + 4)
                    products_scaled(half)
                    add(4 * half, 4 * half + 4)
                    if k == last_heavy:
                        late_stores.append((k, o, 512 * half, 512 * half + 512))
                    else:
                        store(k, o, 512 * half, 512 * half + 512)
                flush(k)
                return
            squares(0)
            nc.vector.tensor_tensor(
                out=pr[:, 0:4, :].rearrange("p h (c a) -> p h c a", a=2),
                in0=tab[0][:].rearrange("p (o c a) -> p o c a", o=1, a=2).to_broadcast([P, 4, D, 2]),
                in1=banks[0][:].rearrange("p (h c o) -> p h c o", h=4, o=1).to_broadcast([P, 4, D, 2]),
                op=ALU.mult,
            )
            squares(1)
            rstd(0, 8)
            products_scaled(1)
            flush(k)
            add(0, 8)
            pending.append((k, finish))

        for k in range(len(groups)):
            banks = matmuls(k)
            if groups[k][0] == 2:
                light(k, banks)
            else:
                heavy_group(k, banks)
            if k == 1:
                load_text_x()
                load_text_w(0)
            if k == 3:
                load_text_w(1)
            if k == 5:
                load_text_w(2)
